import numpy as np
import ml_dtypes


def mxq(x, axis, fmt="e4m3"):
    dtype, down = {"e4m3": (ml_dtypes.float8_e4m3fn, 7), "e5m2": (ml_dtypes.float8_e5m2, 14)}[fmt]
    v = np.moveaxis(np.asarray(x, np.float32).astype(ml_dtypes.bfloat16).astype(np.float64), axis, -1)
    blocks = v.reshape(v.shape[:-1] + (-1, 32))
    amax = np.abs(blocks).max(-1, keepdims=True)
    byte = np.maximum(np.where(amax > 0, np.frexp(amax)[1] - 1 + 127, 0) - down, 1)
    scale = np.exp2(byte - 127.0)
    codes = (blocks / scale).astype(np.float32).astype(dtype).astype(np.float64)
    return np.moveaxis((codes * scale).reshape(v.shape), -1, axis)


WIDE = False


def mx_kscale(k):
    if not WIDE:
        return np.ones(k)
    levels = np.array([10, -10, 5, -5, 0])
    if k % 512:
        return np.exp2(np.random.permutation(np.resize(levels, k // 32))).repeat(32)
    a = np.empty((k // 512, 16))
    for p in range(k // 512):
        a[p, :8] = np.random.permutation(np.resize(levels, 8))
        for g in range(8):
            far = levels[np.abs(levels - a[p, g]) >= 10]
            a[p, g + 8] = far[np.random.randint(len(far))]
    return np.exp2(a.ravel()).repeat(32)


BF16 = ml_dtypes.bfloat16


def bf(x):
    return np.asarray(x, np.float32).astype(BF16)


def f64(x):
    return np.asarray(x).astype(np.float64)


B, S, H, NH, NKV, HD = 4, 2048, 1024, 2, 1, 128
EPS = 1e-6


def rms_norm(x, w):
    var = np.mean(x * x, axis=-1, keepdims=True)
    return x * (1.0 / np.sqrt(var + EPS)) * w


def rotate_half(x):
    x1, x2 = np.split(x, 2, axis=-1)
    return np.concatenate([-x2, x1], axis=-1)


def setup_inputs():
    s = mx_kscale(H)
    inv_freq = 1.0 / (10000.0 ** (np.arange(0, HD, 2) / HD))
    freqs = np.arange(S)[:, None] * inv_freq[None, :]
    emb = np.concatenate([freqs, freqs], axis=-1)
    return {"hidden_states": bf(np.random.standard_normal((B, S, H)) * s),
            "cos": bf(np.cos(emb)),
            "sin": bf(np.sin(emb)),
            "wq": bf(np.random.standard_normal((NH * HD, H)) / np.sqrt(H) / s[None, :]),
            "wk": bf(np.random.standard_normal((NKV * HD, H)) / np.sqrt(H) / s[None, :]),
            "q_norm_w": bf(1.0 + 0.1 * np.random.standard_normal(HD)),
            "k_norm_w": bf(1.0 + 0.1 * np.random.standard_normal(HD)),
            "ssmax_scale": bf((1.0 + 0.2 * np.random.standard_normal((1, NH, 1, 1))) / np.log(S))}


def reference(hidden_states, cos, sin, wq, wk, q_norm_w, k_norm_w, ssmax_scale):
    xq = mxq(f64(hidden_states), 2, "e4m3")
    q = (xq @ mxq(f64(wq), 1, "e4m3").T).reshape(B, S, NH, HD)
    k = (xq @ mxq(f64(wk), 1, "e4m3").T).reshape(B, S, NKV, HD)
    q = rms_norm(q, f64(q_norm_w)).transpose(0, 2, 1, 3)
    k = rms_norm(k, f64(k_norm_w)).transpose(0, 2, 1, 3)
    c = f64(cos)[None, None]
    sn = f64(sin)[None, None]
    q = q * c + rotate_half(q) * sn
    k = k * c + rotate_half(k) * sn
    q = q * (f64(ssmax_scale) * np.log(S))
    return q, k

@@ -1,0 +1,321 @@
+import math
+from contextlib import ExitStack
+
+import concourse.mybir as mybir
+from concourse.masks import make_identity
+
+F32 = mybir.dt.float32
+BF16 = mybir.dt.bfloat16
+U32 = mybir.dt.uint32
+U8 = mybir.dt.uint8
+FP8X4 = mybir.dt.float8_e4m3fn_x4
+ALU = mybir.AluOpType
+ACT = mybir.ActivationFunctionType
+
+P = 128
+BATCH = 4
+SEQ = 2048
+HIDDEN = 1024
+Q_HEADS = 2
+HEADS = 3
+HD = 128
+HALF = HD // 2
+EPS = 1e-6
+
+K_PASS = 4 * P
+PASSES = HIDDEN // K_PASS
+WORDS = HIDDEN // 2
+BLOCKS = WORDS // P
+SLICES = SEQ // P
+GROUP = 4
+UNIT = 2
+CHUNKS = SLICES // GROUP
+GROUPS = CHUNKS * BATCH
+UNITS_PER_GROUP = GROUP // UNIT
+UNITS_PER_CHUNK = BATCH * UNITS_PER_GROUP
+UNITS = GROUPS * UNITS_PER_GROUP
+LOAD_AHEAD = 10
+HEAD_CHUNK = 1
+QUANTISE_LAG = 1
+PROJECT_LAG = 2
+ROTATE_LAG = 3
+
+FLOPS = 2 * BATCH * SEQ * HIDDEN * HEADS * HD
+
+
+def transpose_rows(nc, psum_t, ident, words):
+    bank = psum_t.tile([P, WORDS], F32, name="bank")
+    for j in range(BLOCKS):
+        g, u = divmod(j, 2)
+        nc.tensor.transpose(
+            bank[:, j * P : (j + 1) * P], words[:, 2 * g * P + u : 2 * (g + 1) * P : 2], ident[:]
+        )
+    return bank
+
+
+def copy_grouped(nc, bank, grouped_words):
+    nc.scalar.copy(
+        out=grouped_words,
+        in_=bank[:].rearrange("p (g u r) -> p g r u", g=PASSES, u=2),
+    )
+
+
+def tile_biboattention_pa_t_kernel(
+    tc, hidden_states, cos, sin, wq, wk, q_norm_w, k_norm_w, ssmax_scale, out_0, out_1
+):
+    nc = tc.nc
+    with ExitStack() as ctx:
+        const = ctx.enter_context(tc.tile_pool(name="const", bufs=1))
+        x_pool = ctx.enter_context(tc.tile_pool(name="x", bufs=LOAD_AHEAD + 1))
+        angle_pool = ctx.enter_context(tc.tile_pool(name="angle", bufs=CHUNKS))
+        table_pool = ctx.enter_context(tc.tile_pool(name="table", bufs=2))
+        mx_pool = ctx.enter_context(tc.tile_pool(name="mx", bufs=3))
+        stat_pool = ctx.enter_context(tc.tile_pool(name="stat", bufs=4))
+        prod_pool = ctx.enter_context(tc.tile_pool(name="prod", bufs=3))
+        out_pool = ctx.enter_context(tc.tile_pool(name="out", bufs=3))
+        psum_t = ctx.enter_context(tc.psum_pool(name="psum_t", bufs=UNIT))
+        psum_o = ctx.enter_context(tc.psum_pool(name="psum_o", bufs=2 * UNIT))
+        psum_w = ctx.enter_context(tc.psum_pool(name="psum_w", bufs=1))
+        ctx.enter_context(tc.manual_schedule())
+
+        cos_slices = cos.rearrange("(p t) d -> p t d", t=SLICES)
+        sin_slices = sin.rearrange("(p t) d -> p t d", t=SLICES)
+
+        angles = {}
+        tables = {}
+        x_words = {}
+        banks = {}
+        groupeds = {}
+        operands = {}
+        raws = {}
+        rstds = {}
+        products = {}
+        results = {}
+
+        def group_slices(n):
+            chunk = n // BATCH
+            return slice(chunk * GROUP, (chunk + 1) * GROUP)
+
+        def load_angles(chunk):
+            angle = angle_pool.tile([P, 2, GROUP, HD], BF16)
+            nc.sync.dma_start(out=angle[:, 0], in_=cos_slices[:, group_slices(chunk * BATCH), :])
+            nc.sync.dma_start(out=angle[:, 1], in_=sin_slices[:, group_slices(chunk * BATCH), :])
+            angles[chunk] = angle
+
+        def build_tables(engine, for_cos, for_sin, chunk, v):
+            if v == 0:
+                tables[chunk] = table_pool.tile([P, GROUP, HEADS, 2, HD], F32, name="table")
+            table = tables[chunk]
+            angle = angles[chunk]
+            mine = slice(v * UNIT, (v + 1) * UNIT)
+            engine.tensor_tensor(
+                out=table[:, mine, :, 0, :],
+                in0=angle[:, 0, mine].unsqueeze(2).to_broadcast([P, UNIT, HEADS, HD]),
+                in1=for_cos.unsqueeze(1).to_broadcast([P, UNIT, HEADS, HD]),
+                op=ALU.mult,
+            )
+            for i in range(2):
+                here = slice(i * HALF, (i + 1) * HALF)
+                there = slice((1 - i) * HALF, (2 - i) * HALF)
+                engine.tensor_tensor(
+                    out=table[:, mine, :, 1, here],
+                    in0=angle[:, 1, mine, there].unsqueeze(2).to_broadcast([P, UNIT, HEADS, HALF]),
+                    in1=for_sin[:, :, here].unsqueeze(1).to_broadcast([P, UNIT, HEADS, HALF]),
+                    op=ALU.mult,
+                )
+
+        def load_rows(u):
+            n = u // UNITS_PER_GROUP
+            first = (n // BATCH) * GROUP + (u % UNITS_PER_GROUP) * UNIT
+            x_rows = x_pool.tile([P, UNIT * HIDDEN], BF16)
+            nc.sync.dma_start(
+                out=x_rows[:].rearrange("p (t k) -> p t k", t=UNIT),
+                in_=hidden_states[n % BATCH].rearrange("(p t) k -> p t k", t=SLICES)[:, first : first + UNIT, :],
+            )
+            x_words[u] = x_rows[:].bitcast(F32)
+
+        def transpose_unit(u):
+            banks[u] = [
+                transpose_rows(nc, psum_t, ident, x_words[u][:, s * WORDS : (s + 1) * WORDS])
+                for s in range(UNIT)
+            ]
+
+        def copy_unit(u):
+            grouped = mx_pool.tile([P, UNIT * HIDDEN], BF16, align_bytes=64)
+            grouped_words = grouped[:].bitcast(F32).rearrange(
+                "p (s g r u) -> p s g r u", s=UNIT, g=PASSES, u=2
+            )
+            for s in range(UNIT):
+                copy_grouped(nc, banks[u][s], grouped_words[:, s])
+            groupeds[u] = grouped
+
+        def quantise_unit(u):
+            codes = mx_pool.tile([P, UNIT * PASSES * P], U32, align_bytes=64)
+            scales = mx_pool.tile([P, UNIT * PASSES * P], U8, align_bytes=64)
+            nc.vector.quantize_mx(out=codes[:].bitcast(FP8X4), scales=scales[:], in_=groupeds[u][:])
+            operands[u] = (codes, scales)
+
+        def project_unit(u):
+            codes, scales = operands[u]
+            raws[u] = []
+            for s in range(UNIT):
+                raw = psum_o.tile([P, HEADS * HD], F32)
+                for cols, w_codes, w_scales, width in projections:
+                    for g in range(PASSES):
+                        tokens = slice((s * PASSES + g) * P, (s * PASSES + g + 1) * P)
+                        features = slice(g * width, (g + 1) * width)
+                        nc.tensor.matmul_mx(
+                            out=raw[:, cols],
+                            lhsT=codes[:, tokens].bitcast(FP8X4),
+                            lhsT_scale=scales[:, tokens],
+                            rhs=w_codes[:, features].bitcast(FP8X4),
+                            rhs_scale=w_scales[:, features],
+                            start=(g == 0),
+                            stop=(g == PASSES - 1),
+                        )
+                raws[u].append(raw)
+
+        def norm_unit(u):
+            sumsq = stat_pool.tile([P, UNIT * HEADS], F32)
+            for s in range(UNIT):
+                squares = stat_pool.tile([P, HEADS * HD], BF16)
+                for h in range(HEADS):
+                    head = slice(h * HD, (h + 1) * HD)
+                    nc.scalar.activation(
+                        out=squares[:, head],
+                        in_=raws[u][s][:, head],
+                        func=ACT.Square,
+                        accum_out=sumsq[:, s * HEADS + h : s * HEADS + h + 1],
+                    )
+            rstd = stat_pool.tile([P, UNIT * HEADS], F32)
+            nc.scalar.activation(
+                out=rstd[:], in_=sumsq[:], func=ACT.Abs_reciprocal_sqrt, bias=eps[:], scale=1.0 / HD
+            )
+            rstds[u] = rstd
+
+        def rotate_unit(u):
+            table = tables[u // UNITS_PER_CHUNK]
+            first = (u % UNITS_PER_GROUP) * UNIT
+            product = prod_pool.tile([P, HEADS, UNIT, 2, HD], F32)
+            for s in range(UNIT):
+                for h in range(HEADS):
+                    nc.vector.scalar_tensor_tensor(
+                        out=product[:, h, s],
+                        in0=raws[u][s][:, h * HD : (h + 1) * HD].unsqueeze(1).to_broadcast([P, 2, HD]),
+                        scalar=rstds[u][:, s * HEADS + h : s * HEADS + h + 1],
+                        in1=table[:, first + s, h],
+                        op0=ALU.mult,
+                        op1=ALU.mult,
+                    )
+            products[u] = product
+
+        def add_unit(u):
+            n = u // UNITS_PER_GROUP
+            first = (u % UNITS_PER_GROUP) * UNIT
+            if first == 0:
+                results[n] = out_pool.tile([P, HEADS, GROUP, HD], F32, name="result")
+            halves = products[u][:].rearrange("p h s a (i d) -> p h s a i d", i=2)
+            nc.gpsimd.tensor_tensor(
+                out=results[n][:, :, first : first + UNIT, :].rearrange("p h s (i d) -> p h s i d", i=2),
+                in0=halves[:, :, :, 0],
+                in1=halves[:, :, :, 1, ::-1],
+                op=ALU.add,
+            )
+
+        def store_group(n):
+            b = n % BATCH
+            nc.sync.dma_start(
+                out=out_0[b].rearrange("h (p t) d -> p h t d", t=SLICES)[:, :, group_slices(n), :],
+                in_=results[n][:, 0:Q_HEADS],
+            )
+            nc.sync.dma_start(
+                out=out_1[b, 0].rearrange("(p t) d -> p t d", t=SLICES)[:, group_slices(n), :],
+                in_=results[n][:, Q_HEADS],
+            )
+
+        wq_rows = const.tile([P, HD], BF16)
+        wk_rows = const.tile([P, HD], BF16)
+        gain_rows = const.tile([P, Q_HEADS], BF16)
+        nc.scalar.dma_start(out=wq_rows[:], in_=q_norm_w.partition_broadcast(P))
+        nc.scalar.dma_start(out=wk_rows[:], in_=k_norm_w.partition_broadcast(P))
+        nc.scalar.dma_start(
+            out=gain_rows[:], in_=ssmax_scale.rearrange("a h b c -> (a h b c)").partition_broadcast(P)
+        )
+        w_raw = const.tile([P, HEADS, HIDDEN], BF16)
+        nc.sync.dma_start(out=w_raw[:, 0:Q_HEADS, :], in_=wq.rearrange("(a p) k -> p a k", p=P))
+        nc.sync.dma_start(out=w_raw[:, Q_HEADS, :], in_=wk)
+        load_rows(0)
+        load_angles(0)
+        load_angles(HEAD_CHUNK)
+        for u in range(1, LOAD_AHEAD):
+            load_rows(u)
+        for chunk in range(HEAD_CHUNK + 1, CHUNKS):
+            load_angles(chunk)
+
+        ident = const.tile([P, P], F32)
+        make_identity(nc, ident[:])
+        eps = const.tile([P, 1], F32)
+        nc.vector.memset(eps[:], EPS)
+        warm = const.tile([P, 1], F32)
+        nc.scalar.activation(out=warm[:], in_=eps[:], func=ACT.Abs_reciprocal_sqrt)
+
+        gain = const.tile([P, Q_HEADS], F32)
+        nc.vector.tensor_scalar_mul(out=gain[:], in0=gain_rows[:], scalar1=math.log(SEQ))
+        w_cos = const.tile([P, HEADS, HD], F32)
+        for h in range(Q_HEADS):
+            nc.vector.tensor_scalar_mul(out=w_cos[:, h, :], in0=wq_rows[:], scalar1=gain[:, h : h + 1])
+        nc.vector.tensor_copy(out=w_cos[:, Q_HEADS, :], in_=wk_rows[:])
+        w_sin = const.tile([P, HEADS, HD], F32)
+        nc.vector.tensor_copy(out=w_sin[:, :, 0:HALF], in_=w_cos[:, :, 0:HALF])
+        nc.vector.tensor_scalar_mul(out=w_sin[:, :, HALF:HD], in0=w_cos[:, :, HALF:HD], scalar1=-1.0)
+        for v in range(UNITS_PER_GROUP):
+            build_tables(nc.gpsimd, w_cos[:], w_sin[:], HEAD_CHUNK, v)
+
+        wq_grouped = const.tile([P, PASSES * Q_HEADS * HD * 4], BF16, align_bytes=64)
+        wk_grouped = const.tile([P, PASSES * HD * 4], BF16, align_bytes=64)
+        wq_words = wq_grouped[:].bitcast(F32).rearrange("p (g n u) -> p g n u", g=PASSES, u=2)
+        wk_words = wk_grouped[:].bitcast(F32).rearrange("p (g n u) -> p g n u", g=PASSES, u=2)
+        for h in range(HEADS):
+            bank = transpose_rows(nc, psum_t, ident, w_raw[:, h, :].bitcast(F32))
+            if h < Q_HEADS:
+                copy_grouped(nc, bank, wq_words[:, :, h * HD : (h + 1) * HD, :])
+            else:
+                copy_grouped(nc, bank, wk_words)
+        wq_codes = const.tile([P, PASSES * Q_HEADS * HD], U32, align_bytes=64)
+        wq_scales = const.tile([P, PASSES * Q_HEADS * HD], U8, align_bytes=64)
+        wk_codes = const.tile([P, PASSES * HD], U32, align_bytes=64)
+        wk_scales = const.tile([P, PASSES * HD], U8, align_bytes=64)
+        nc.vector.quantize_mx(out=wq_codes[:].bitcast(FP8X4), scales=wq_scales[:], in_=wq_grouped[:])
+        nc.vector.quantize_mx(out=wk_codes[:].bitcast(FP8X4), scales=wk_scales[:], in_=wk_grouped[:])
+        projections = (
+            (slice(0, Q_HEADS * HD), wq_codes, wq_scales, Q_HEADS * HD),
+            (slice(Q_HEADS * HD, HEADS * HD), wk_codes, wk_scales, HD),
+        )
+
+        w_cos_psum = psum_w.tile([P, HEADS, HD], F32)
+        w_sin_psum = psum_w.tile([P, HEADS, HD], F32)
+
+        for step in range(UNITS + ROTATE_LAG):
+            if step + LOAD_AHEAD < UNITS:
+                load_rows(step + LOAD_AHEAD)
+            if step < UNITS:
+                transpose_unit(step)
+                copy_unit(step)
+            if step == 0:
+                nc.tensor.matmul(out=w_cos_psum[:], lhsT=ident[:], rhs=w_cos[:], start=True, stop=True)
+                nc.tensor.matmul(out=w_sin_psum[:], lhsT=ident[:], rhs=w_sin[:], start=True, stop=True)
+            if 0 <= step - QUANTISE_LAG < UNITS:
+                fresh = step - QUANTISE_LAG
+                quantise_unit(fresh)
+                chunk, v = divmod(fresh, UNITS_PER_CHUNK)
+                if v < UNITS_PER_GROUP and chunk != HEAD_CHUNK:
+                    build_tables(nc.vector, w_cos_psum[:], w_sin_psum[:], chunk, v)
+            if 0 <= step - PROJECT_LAG < UNITS:
+                project_unit(step - PROJECT_LAG)
+                norm_unit(step - PROJECT_LAG)
+            if 0 <= step - ROTATE_LAG:
+                done = step - ROTATE_LAG
+                rotate_unit(done)
+                add_unit(done)
+                if done % UNITS_PER_GROUP == UNITS_PER_GROUP - 1:
+                    store_group(done // UNITS_PER_GROUP)

@@ -35,10 +35,9 @@ UNITS_PER_GROUP = GROUP // UNIT
 UNITS_PER_CHUNK = BATCH * UNITS_PER_GROUP
 UNITS = GROUPS * UNITS_PER_GROUP
 LOAD_AHEAD = 10
-HEAD_CHUNK = 1
-QUANTISE_LAG = 1
+G_CHUNK = 1
 PROJECT_LAG = 2
-ROTATE_LAG = 3
+NORMS = 2
 
 FLOPS = 2 * BATCH * SEQ * HIDDEN * HEADS * HD
 
@@ -53,8 +52,8 @@ def transpose_rows(nc, psum_t, ident, words):
     return bank
 
 
-def copy_grouped(nc, bank, grouped_words):
-    nc.scalar.copy(
+def copy_grouped(copy, bank, grouped_words):
+    copy(
         out=grouped_words,
         in_=bank[:].rearrange("p (g u r) -> p g r u", g=PASSES, u=2),
     )
@@ -68,13 +67,13 @@ def tile_biboattention_pa_t_kernel(
         const = ctx.enter_context(tc.tile_pool(name="const", bufs=1))
         x_pool = ctx.enter_context(tc.tile_pool(name="x", bufs=LOAD_AHEAD + 1))
         angle_pool = ctx.enter_context(tc.tile_pool(name="angle", bufs=CHUNKS))
-        table_pool = ctx.enter_context(tc.tile_pool(name="table", bufs=2))
-        mx_pool = ctx.enter_context(tc.tile_pool(name="mx", bufs=3))
+        table_pool = ctx.enter_context(tc.tile_pool(name="table", bufs=CHUNKS))
+        mx_pool = ctx.enter_context(tc.tile_pool(name="mx", bufs=4))
         stat_pool = ctx.enter_context(tc.tile_pool(name="stat", bufs=4))
-        prod_pool = ctx.enter_context(tc.tile_pool(name="prod", bufs=3))
+        prod_pool = ctx.enter_context(tc.tile_pool(name="prod", bufs=4))
         out_pool = ctx.enter_context(tc.tile_pool(name="out", bufs=3))
-        psum_t = ctx.enter_context(tc.psum_pool(name="psum_t", bufs=UNIT))
-        psum_o = ctx.enter_context(tc.psum_pool(name="psum_o", bufs=2 * UNIT))
+        psum_t = ctx.enter_context(tc.psum_pool(name="psum_t", bufs=3))
+        psum_o = ctx.enter_context(tc.psum_pool(name="psum_o", bufs=4))
         psum_w = ctx.enter_context(tc.psum_pool(name="psum_w", bufs=1))
         ctx.enter_context(tc.manual_schedule())
 
@@ -88,6 +87,7 @@ def tile_biboattention_pa_t_kernel(
         groupeds = {}
         operands = {}
         raws = {}
+        sumsqs = {}
         rstds = {}
         products = {}
         results = {}
@@ -102,52 +102,76 @@ def tile_biboattention_pa_t_kernel(
             nc.sync.dma_start(out=angle[:, 1], in_=sin_slices[:, group_slices(chunk * BATCH), :])
             angles[chunk] = angle
 
-        def build_tables(engine, for_cos, for_sin, chunk, v):
-            if v == 0:
-                tables[chunk] = table_pool.tile([P, GROUP, HEADS, 2, HD], F32, name="table")
-            table = tables[chunk]
-            angle = angles[chunk]
-            mine = slice(v * UNIT, (v + 1) * UNIT)
+        def table_part(chunk, part, t0, t1):
+            if chunk not in tables:
+                tables[chunk] = table_pool.tile([P, GROUP, NORMS, 2, HD], F32, name="table")
+            table, angle = tables[chunk], angles[chunk]
+            if part == 0:
+                return table[:, t0:t1, :, 0], angle[:, 0, t0:t1]
+            here = slice((part - 1) * HALF, part * HALF)
+            there = slice((2 - part) * HALF, (3 - part) * HALF)
+            return table[:, t0:t1, :, 1, here], angle[:, 1, t0:t1, there]
+
+        def table_product(engine, out, w, angle):
+            shape = [P, out.shape[1], NORMS, out.shape[3]]
             engine.tensor_tensor(
-                out=table[:, mine, :, 0, :],
-                in0=angle[:, 0, mine].unsqueeze(2).to_broadcast([P, UNIT, HEADS, HD]),
-                in1=for_cos.unsqueeze(1).to_broadcast([P, UNIT, HEADS, HD]),
+                out=out,
+                in0=w.unsqueeze(1).to_broadcast(shape),
+                in1=angle.unsqueeze(2).to_broadcast(shape),
                 op=ALU.mult,
             )
-            for i in range(2):
-                here = slice(i * HALF, (i + 1) * HALF)
-                there = slice((1 - i) * HALF, (2 - i) * HALF)
-                engine.tensor_tensor(
-                    out=table[:, mine, :, 1, here],
-                    in0=angle[:, 1, mine, there].unsqueeze(2).to_broadcast([P, UNIT, HEADS, HALF]),
-                    in1=for_sin[:, :, here].unsqueeze(1).to_broadcast([P, UNIT, HEADS, HALF]),
-                    op=ALU.mult,
-                )
 
-        def load_rows(u):
+        def build_tables_gpsimd(chunk, v):
+            for part, w in enumerate((w_rows[:], w_rows[:, :, 0:HALF], w_minus[:])):
+                out, angle = table_part(chunk, part, v * UNIT, (v + 1) * UNIT)
+                table_product(nc.gpsimd, out, w, angle)
+
+        def build_tables(chunk, t0, t1, parts=(0, 1, 2)):
+            for part in parts:
+                if part < 2:
+                    out, angle = table_part(chunk, part, t0, t1)
+                    table_product(nc.vector, out, w_psum if part == 0 else w_psum[:, :, 0:HALF], angle)
+                    continue
+                for t in range(t0, t1):
+                    out, angle = table_part(chunk, part, t, t + 1)
+                    nc.vector.scalar_tensor_tensor(
+                        out=out[:, 0],
+                        in0=w_psum[:, :, HALF:HD],
+                        scalar=-1.0,
+                        in1=angle.to_broadcast([P, NORMS, HALF]),
+                        op0=ALU.mult,
+                        op1=ALU.mult,
+                    )
+
+        def load_rows(u, parts=1):
             n = u // UNITS_PER_GROUP
             first = (n // BATCH) * GROUP + (u % UNITS_PER_GROUP) * UNIT
             x_rows = x_pool.tile([P, UNIT * HIDDEN], BF16)
-            nc.sync.dma_start(
-                out=x_rows[:].rearrange("p (t k) -> p t k", t=UNIT),
-                in_=hidden_states[n % BATCH].rearrange("(p t) k -> p t k", t=SLICES)[:, first : first + UNIT, :],
+            views = (
+                x_rows[:].rearrange("p (t k) -> p t k", t=UNIT),
+                hidden_states[n % BATCH].rearrange("(p t) k -> p t k", t=SLICES)[:, first : first + UNIT, :],
             )
+            step = UNIT // parts
+            for t in range(0, UNIT, step):
+                nc.sync.dma_start(out=views[0][:, t : t + step], in_=views[1][:, t : t + step])
             x_words[u] = x_rows[:].bitcast(F32)
 
-        def transpose_unit(u):
-            banks[u] = [
-                transpose_rows(nc, psum_t, ident, x_words[u][:, s * WORDS : (s + 1) * WORDS])
-                for s in range(UNIT)
-            ]
+        def transpose_slice(u, s):
+            if s == 0:
+                banks[u] = []
+            banks[u].append(transpose_rows(nc, psum_t, ident, x_words[u][:, s * WORDS : (s + 1) * WORDS]))
 
-        def copy_unit(u):
-            grouped = mx_pool.tile([P, UNIT * HIDDEN], BF16, align_bytes=64)
-            grouped_words = grouped[:].bitcast(F32).rearrange(
+        def transpose_unit(u):
+            for s in range(UNIT):
+                transpose_slice(u, s)
+
+        def copy_slice(u, s, copy):
+            if s == 0:
+                groupeds[u] = mx_pool.tile([P, UNIT * HIDDEN], BF16, align_bytes=64, name="grouped")
+            grouped_words = groupeds[u][:].bitcast(F32).rearrange(
                 "p (s g r u) -> p s g r u", s=UNIT, g=PASSES, u=2
             )
-            for s in range(UNIT):
-                copy_grouped(nc, banks[u][s], grouped_words[:, s])
-            groupeds[u] = grouped
+            copy_grouped(copy, banks[u][s], grouped_words[:, s])
 
         def quantise_unit(u):
             codes = mx_pool.tile([P, UNIT * PASSES * P], U32, align_bytes=64)
@@ -175,9 +199,11 @@ def tile_biboattention_pa_t_kernel(
                         )
                 raws[u].append(raw)
 
-        def norm_unit(u):
-            sumsq = stat_pool.tile([P, UNIT * HEADS], F32)
-            for s in range(UNIT):
+        def square_unit(u, slices=range(UNIT)):
+            if slices[0] == 0:
+                sumsqs[u] = stat_pool.tile([P, HEADS, UNIT], F32, name="sumsq")
+            sumsq = sumsqs[u]
+            for s in slices:
                 squares = stat_pool.tile([P, HEADS * HD], BF16)
                 for h in range(HEADS):
                     head = slice(h * HD, (h + 1) * HD)
@@ -185,11 +211,13 @@ def tile_biboattention_pa_t_kernel(
                         out=squares[:, head],
                         in_=raws[u][s][:, head],
                         func=ACT.Square,
-                        accum_out=sumsq[:, s * HEADS + h : s * HEADS + h + 1],
+                        accum_out=sumsq[:, h, s : s + 1],
                     )
-            rstd = stat_pool.tile([P, UNIT * HEADS], F32)
+
+        def norm_unit(u):
+            rstd = stat_pool.tile([P, HEADS, UNIT], F32)
             nc.scalar.activation(
-                out=rstd[:], in_=sumsq[:], func=ACT.Abs_reciprocal_sqrt, bias=eps[:], scale=1.0 / HD
+                out=rstd[:], in_=sumsqs[u][:], func=ACT.Abs_reciprocal_sqrt, bias=eps[:], scale=1.0 / HD
             )
             rstds[u] = rstd
 
@@ -197,125 +225,170 @@ def tile_biboattention_pa_t_kernel(
             table = tables[u // UNITS_PER_CHUNK]
             first = (u % UNITS_PER_GROUP) * UNIT
             product = prod_pool.tile([P, HEADS, UNIT, 2, HD], F32)
-            for s in range(UNIT):
-                for h in range(HEADS):
+            factor = stat_pool.tile([P, Q_HEADS, UNIT], F32)
+            nc.vector.tensor_tensor(out=factor[:], in0=gain_psum, in1=rstds[u][:, 0:Q_HEADS], op=ALU.mult)
+            factors = [factor[:, 0], factor[:, 1], rstds[u][:, Q_HEADS]]
+            for h in (2, 0, 1):
+                for s in range(UNIT):
                     nc.vector.scalar_tensor_tensor(
                         out=product[:, h, s],
                         in0=raws[u][s][:, h * HD : (h + 1) * HD].unsqueeze(1).to_broadcast([P, 2, HD]),
-                        scalar=rstds[u][:, s * HEADS + h : s * HEADS + h + 1],
-                        in1=table[:, first + s, h],
+                        scalar=factors[h][:, s : s + 1],
+                        in1=table[:, first + s, h // Q_HEADS],
                         op0=ALU.mult,
                         op1=ALU.mult,
                     )
             products[u] = product
 
-        def add_unit(u):
+        def add_slices(engine, u, s0, s1):
             n = u // UNITS_PER_GROUP
             first = (u % UNITS_PER_GROUP) * UNIT
-            if first == 0:
+            if first + s0 == 0:
                 results[n] = out_pool.tile([P, HEADS, GROUP, HD], F32, name="result")
-            halves = products[u][:].rearrange("p h s a (i d) -> p h s a i d", i=2)
-            nc.gpsimd.tensor_tensor(
-                out=results[n][:, :, first : first + UNIT, :].rearrange("p h s (i d) -> p h s i d", i=2),
-                in0=halves[:, :, :, 0],
-                in1=halves[:, :, :, 1, ::-1],
+            terms = products[u][:, :, s0:s1].rearrange("p h s a (i d) -> p h s a i d", i=2)
+            engine.tensor_tensor(
+                out=results[n][:, :, first + s0 : first + s1, :].rearrange("p h s (i d) -> p h s i d", i=2),
+                in0=terms[:, :, :, 0],
+                in1=terms[:, :, :, 1, ::-1],
                 op=ALU.add,
             )
 
-        def store_group(n):
+        def store(n, t0, t1):
             b = n % BATCH
+            first = group_slices(n).start
             nc.sync.dma_start(
-                out=out_0[b].rearrange("h (p t) d -> p h t d", t=SLICES)[:, :, group_slices(n), :],
-                in_=results[n][:, 0:Q_HEADS],
+                out=out_0[b].rearrange("h (p t) d -> p h t d", t=SLICES)[:, :, first + t0 : first + t1, :],
+                in_=results[n][:, 0:Q_HEADS, t0:t1],
             )
             nc.sync.dma_start(
-                out=out_1[b, 0].rearrange("(p t) d -> p t d", t=SLICES)[:, group_slices(n), :],
-                in_=results[n][:, Q_HEADS],
+                out=out_1[b, 0].rearrange("(p t) d -> p t d", t=SLICES)[:, first + t0 : first + t1, :],
+                in_=results[n][:, Q_HEADS, t0:t1],
             )
 
-        wq_rows = const.tile([P, HD], BF16)
-        wk_rows = const.tile([P, HD], BF16)
+        def copy_weight(h, copy):
+            bank = transpose_rows(nc, psum_t, ident, w_raw[:, h].bitcast(F32))
+            if h < Q_HEADS:
+                copy_grouped(copy, bank, wq_words[:, :, h * HD : (h + 1) * HD, :])
+            else:
+                copy_grouped(copy, bank, wk_words)
+
+        w_raw = const.tile([P, HEADS, HIDDEN], BF16)
+        for h in range(Q_HEADS):
+            nc.sync.dma_start(out=w_raw[:, h], in_=wq[h * HD : (h + 1) * HD, :])
+        nc.sync.dma_start(out=w_raw[:, Q_HEADS], in_=wk)
+        w_rows = const.tile([P, NORMS, HD], BF16)
+        nc.scalar.dma_start(out=w_rows[:, 0], in_=q_norm_w.partition_broadcast(P))
+        nc.scalar.dma_start(out=w_rows[:, 1], in_=k_norm_w.partition_broadcast(P))
         gain_rows = const.tile([P, Q_HEADS], BF16)
-        nc.scalar.dma_start(out=wq_rows[:], in_=q_norm_w.partition_broadcast(P))
-        nc.scalar.dma_start(out=wk_rows[:], in_=k_norm_w.partition_broadcast(P))
         nc.scalar.dma_start(
             out=gain_rows[:], in_=ssmax_scale.rearrange("a h b c -> (a h b c)").partition_broadcast(P)
         )
-        w_raw = const.tile([P, HEADS, HIDDEN], BF16)
-        nc.sync.dma_start(out=w_raw[:, 0:Q_HEADS, :], in_=wq.rearrange("(a p) k -> p a k", p=P))
-        nc.sync.dma_start(out=w_raw[:, Q_HEADS, :], in_=wk)
-        load_rows(0)
+        load_rows(0, UNIT)
         load_angles(0)
-        load_angles(HEAD_CHUNK)
-        for u in range(1, LOAD_AHEAD):
+        for u in range(1, 4):
             load_rows(u)
-        for chunk in range(HEAD_CHUNK + 1, CHUNKS):
+        load_angles(G_CHUNK)
+        for u in range(4, LOAD_AHEAD):
+            load_rows(u)
+        for chunk in range(G_CHUNK + 1, CHUNKS):
             load_angles(chunk)
-
         ident = const.tile([P, P], F32)
         make_identity(nc, ident[:])
         eps = const.tile([P, 1], F32)
         nc.vector.memset(eps[:], EPS)
         warm = const.tile([P, 1], F32)
         nc.scalar.activation(out=warm[:], in_=eps[:], func=ACT.Abs_reciprocal_sqrt)
-
-        gain = const.tile([P, Q_HEADS], F32)
-        nc.vector.tensor_scalar_mul(out=gain[:], in0=gain_rows[:], scalar1=math.log(SEQ))
-        w_cos = const.tile([P, HEADS, HD], F32)
-        for h in range(Q_HEADS):
-            nc.vector.tensor_scalar_mul(out=w_cos[:, h, :], in0=wq_rows[:], scalar1=gain[:, h : h + 1])
-        nc.vector.tensor_copy(out=w_cos[:, Q_HEADS, :], in_=wk_rows[:])
-        w_sin = const.tile([P, HEADS, HD], F32)
-        nc.vector.tensor_copy(out=w_sin[:, :, 0:HALF], in_=w_cos[:, :, 0:HALF])
-        nc.vector.tensor_scalar_mul(out=w_sin[:, :, HALF:HD], in0=w_cos[:, :, HALF:HD], scalar1=-1.0)
-        for v in range(UNITS_PER_GROUP):
-            build_tables(nc.gpsimd, w_cos[:], w_sin[:], HEAD_CHUNK, v)
-
+        ident_bf16 = const.tile([P, P], BF16)
+        nc.vector.tensor_copy(out=ident_bf16[:], in_=ident[:])
+        row = const.tile([P, Q_HEADS * UNIT], F32)
+        nc.vector.tensor_scalar_mul(
+            out=row[:].rearrange("p (h s) -> p h s", h=Q_HEADS),
+            in0=gain_rows[:].unsqueeze(2).to_broadcast([P, Q_HEADS, UNIT]),
+            scalar1=math.log(SEQ),
+        )
+        w_minus = const.tile([P, NORMS, HALF], BF16)
+        nc.vector.tensor_scalar_mul(out=w_minus[:], in0=w_rows[:, :, HALF:HD], scalar1=-1.0)
         wq_grouped = const.tile([P, PASSES * Q_HEADS * HD * 4], BF16, align_bytes=64)
         wk_grouped = const.tile([P, PASSES * HD * 4], BF16, align_bytes=64)
         wq_words = wq_grouped[:].bitcast(F32).rearrange("p (g n u) -> p g n u", g=PASSES, u=2)
         wk_words = wk_grouped[:].bitcast(F32).rearrange("p (g n u) -> p g n u", g=PASSES, u=2)
-        for h in range(HEADS):
-            bank = transpose_rows(nc, psum_t, ident, w_raw[:, h, :].bitcast(F32))
-            if h < Q_HEADS:
-                copy_grouped(nc, bank, wq_words[:, :, h * HD : (h + 1) * HD, :])
-            else:
-                copy_grouped(nc, bank, wk_words)
         wq_codes = const.tile([P, PASSES * Q_HEADS * HD], U32, align_bytes=64)
         wq_scales = const.tile([P, PASSES * Q_HEADS * HD], U8, align_bytes=64)
         wk_codes = const.tile([P, PASSES * HD], U32, align_bytes=64)
         wk_scales = const.tile([P, PASSES * HD], U8, align_bytes=64)
-        nc.vector.quantize_mx(out=wq_codes[:].bitcast(FP8X4), scales=wq_scales[:], in_=wq_grouped[:])
-        nc.vector.quantize_mx(out=wk_codes[:].bitcast(FP8X4), scales=wk_scales[:], in_=wk_grouped[:])
         projections = (
             (slice(0, Q_HEADS * HD), wq_codes, wq_scales, Q_HEADS * HD),
             (slice(Q_HEADS * HD, HEADS * HD), wk_codes, wk_scales, HD),
         )
+        copy_weight(0, nc.scalar.copy)
+        copy_weight(1, nc.vector.tensor_copy)
+        copy_weight(2, nc.vector.tensor_copy)
+        nc.vector.quantize_mx(out=wq_codes[:].bitcast(FP8X4), scales=wq_scales[:], in_=wq_grouped[:])
+        nc.vector.quantize_mx(out=wk_codes[:].bitcast(FP8X4), scales=wk_scales[:], in_=wk_grouped[:])
 
-        w_cos_psum = psum_w.tile([P, HEADS, HD], F32)
-        w_sin_psum = psum_w.tile([P, HEADS, HD], F32)
+        def front(u, copies):
+            if u + LOAD_AHEAD < UNITS:
+                load_rows(u + LOAD_AHEAD)
+            transpose_unit(u)
+            for s in range(UNIT):
+                copy_slice(u, s, copies[s])
 
-        for step in range(UNITS + ROTATE_LAG):
-            if step + LOAD_AHEAD < UNITS:
-                load_rows(step + LOAD_AHEAD)
-            if step < UNITS:
-                transpose_unit(step)
-                copy_unit(step)
-            if step == 0:
-                nc.tensor.matmul(out=w_cos_psum[:], lhsT=ident[:], rhs=w_cos[:], start=True, stop=True)
-                nc.tensor.matmul(out=w_sin_psum[:], lhsT=ident[:], rhs=w_sin[:], start=True, stop=True)
-            if 0 <= step - QUANTISE_LAG < UNITS:
-                fresh = step - QUANTISE_LAG
-                quantise_unit(fresh)
-                chunk, v = divmod(fresh, UNITS_PER_CHUNK)
-                if v < UNITS_PER_GROUP and chunk != HEAD_CHUNK:
-                    build_tables(nc.vector, w_cos_psum[:], w_sin_psum[:], chunk, v)
-            if 0 <= step - PROJECT_LAG < UNITS:
-                project_unit(step - PROJECT_LAG)
-                norm_unit(step - PROJECT_LAG)
-            if 0 <= step - ROTATE_LAG:
-                done = step - ROTATE_LAG
-                rotate_unit(done)
-                add_unit(done)
-                if done % UNITS_PER_GROUP == UNITS_PER_GROUP - 1:
-                    store_group(done // UNITS_PER_GROUP)
+        def finish(u):
+            n, v = divmod(u, UNITS_PER_GROUP)
+            rotate_unit(u)
+            if u < UNITS - 1:
+                add_slices(nc.gpsimd, u, 0, UNIT)
+                if n == GROUPS - 1:
+                    store(n, v * UNIT, (v + 1) * UNIT)
+                elif v == UNITS_PER_GROUP - 1:
+                    store(n, 0, GROUP)
+            else:
+                for s in range(UNIT):
+                    add_slices(nc.vector, u, s, s + 1)
+                    store(n, v * UNIT + s, v * UNIT + s + 1)
+
+        front(0, [nc.scalar.copy, nc.vector.tensor_copy])
+        const_bank = psum_w.tile([P, NORMS * HD + Q_HEADS * UNIT], F32)
+        nc.tensor.matmul(
+            out=const_bank[:, 0 : NORMS * HD].rearrange("p (n d) -> p n d", n=NORMS), lhsT=ident_bf16[:], rhs=w_rows[:], start=True, stop=True
+        )
+        nc.tensor.matmul(out=const_bank[:, NORMS * HD :], lhsT=ident[:], rhs=row[:], start=True, stop=True)
+        w_psum = const_bank[:, 0 : NORMS * HD].rearrange("p (n d) -> p n d", n=NORMS)
+        gain_psum = const_bank[:, NORMS * HD :].rearrange("p (h s) -> p h s", h=Q_HEADS)
+        quantise_unit(0)
+        build_tables(0, 0, UNIT)
+        for v in range(UNITS_PER_GROUP):
+            build_tables_gpsimd(G_CHUNK, v)
+        front(1, [nc.scalar.copy, nc.scalar.copy])
+        project_unit(0)
+        square_unit(0)
+        norm_unit(0)
+        quantise_unit(1)
+        for u in range(2, 1 + PROJECT_LAG):
+            front(u, [nc.scalar.copy, nc.scalar.copy])
+        later = [
+            (chunk, t, t + 1, parts) for chunk in range(G_CHUNK + 1, CHUNKS) for t in range(GROUP) for parts in ((0,), (1, 2))
+        ]
+        for u in range(UNITS):
+            ahead = u + 1 + PROJECT_LAG
+            if ahead < UNITS:
+                if ahead + LOAD_AHEAD < UNITS:
+                    load_rows(ahead + LOAD_AHEAD)
+                transpose_unit(ahead)
+                copy_slice(ahead, 0, nc.scalar.copy)
+            if u + 1 < UNITS:
+                project_unit(u + 1)
+            if ahead < UNITS:
+                copy_slice(ahead, 1, nc.scalar.copy)
+            if u + 1 < UNITS:
+                square_unit(u + 1)
+                norm_unit(u + 1)
+            if u + 2 < UNITS and u > 0:
+                quantise_unit(u + 2)
+                i, on = divmod(u - 7, 1)
+                if on == 0 and 0 <= i < len(later):
+                    build_tables(*later[i])
+            finish(u)
+            if u == 0:
+                build_tables(0, UNIT, GROUP)
+                quantise_unit(2)

@@ -88,6 +88,7 @@ def tile_biboattention_pa_t_kernel(
         operands = {}
         raws = {}
         sumsqs = {}
+        turneds = {}
         rstds = {}
         products = {}
         results = {}
@@ -142,6 +143,24 @@ def tile_biboattention_pa_t_kernel(
                         op0=ALU.mult,
                         op1=ALU.mult,
                     )
+
+        def turn_angles(chunk):
+            bank = psum_t.tile([P, 2, GROUP, P], BF16, name="bank")
+            for a in range(2):
+                for t in range(GROUP):
+                    nc.tensor.transpose(bank[:, a, t], angles[chunk][:, a, t], ident_bf16[:])
+            turneds[chunk] = angle_pool.tile([P, 2, GROUP, P], BF16, name="turned")
+            nc.scalar.copy(out=turneds[chunk][:], in_=bank[:])
+
+        def build_table(chunk, t):
+            if chunk not in tables:
+                tables[chunk] = table_pool.tile([P, GROUP, NORMS, 2, HD], F32, name="table")
+            bank = psum_t.tile([P, 2, NORMS, HD], F32, name="bank")
+            for a in range(2):
+                nc.tensor.matmul(
+                    out=bank[:, a], lhsT=turneds[chunk][:, a, t], rhs=weighted[:, a], start=True, stop=True
+                )
+            nc.scalar.copy(out=tables[chunk][:, t], in_=bank[:].rearrange("p a n d -> p n a d"))
 
         def load_rows(u, parts=1):
             n = u // UNITS_PER_GROUP
@@ -228,8 +247,8 @@ def tile_biboattention_pa_t_kernel(
             factor = stat_pool.tile([P, Q_HEADS, UNIT], F32)
             nc.vector.tensor_tensor(out=factor[:], in0=gain_psum, in1=rstds[u][:, 0:Q_HEADS], op=ALU.mult)
             factors = [factor[:, 0], factor[:, 1], rstds[u][:, Q_HEADS]]
-            for h in (2, 0, 1):
-                for s in range(UNIT):
+            for s in range(UNIT):
+                for h in (2, 0, 1):
                     nc.vector.scalar_tensor_tensor(
                         out=product[:, h, s],
                         in0=raws[u][s][:, h * HD : (h + 1) * HD].unsqueeze(1).to_broadcast([P, 2, HD]),
@@ -308,6 +327,18 @@ def tile_biboattention_pa_t_kernel(
         )
         w_minus = const.tile([P, NORMS, HALF], BF16)
         nc.vector.tensor_scalar_mul(out=w_minus[:], in0=w_rows[:, :, HALF:HD], scalar1=-1.0)
+        weighted = const.tile([P, 2, NORMS, HD], BF16)
+        for out, w, there in (
+            (weighted[:, 0], w_rows[:], 0),
+            (weighted[:, 1, :, 0:HALF], w_rows[:, :, 0:HALF], HALF),
+            (weighted[:, 1, :, HALF:HD], w_minus[:], 0),
+        ):
+            nc.gpsimd.tensor_tensor(
+                out=out,
+                in0=w,
+                in1=ident_bf16[:, there : there + w.shape[2]].unsqueeze(1).to_broadcast([P, NORMS, w.shape[2]]),
+                op=ALU.mult,
+            )
         wq_grouped = const.tile([P, PASSES * Q_HEADS * HD * 4], BF16, align_bytes=64)
         wk_grouped = const.tile([P, PASSES * HD * 4], BF16, align_bytes=64)
         wq_words = wq_grouped[:].bitcast(F32).rearrange("p (g n u) -> p g n u", g=PASSES, u=2)
@@ -364,11 +395,17 @@ def tile_biboattention_pa_t_kernel(
         square_unit(0)
         norm_unit(0)
         quantise_unit(1)
+        build_tables(0, UNIT, GROUP)
         for u in range(2, 1 + PROJECT_LAG):
             front(u, [nc.scalar.copy, nc.scalar.copy])
         later = [
-            (chunk, t, t + 1, parts) for chunk in range(G_CHUNK + 1, CHUNKS) for t in range(GROUP) for parts in ((0,), (1, 2))
+            (chunk, t, t + 1, parts) for chunk in [2] for t in range(GROUP) for parts in ((0,), (1, 2))
         ]
+        jobs = {}
+        for i, chunk in enumerate([3]):
+            jobs[8 + i * 2 * (GROUP + 1)] = (turn_angles, (chunk,))
+            for t in range(GROUP):
+                jobs[8 + (i * (GROUP + 1) + t + 1) * 2] = (build_table, (chunk, t))
         for u in range(UNITS):
             ahead = u + 1 + PROJECT_LAG
             if ahead < UNITS:
@@ -383,6 +420,9 @@ def tile_biboattention_pa_t_kernel(
             if u + 1 < UNITS:
                 square_unit(u + 1)
                 norm_unit(u + 1)
+            if u in jobs:
+                job, args = jobs[u]
+                job(*args)
             if u + 2 < UNITS and u > 0:
                 quantise_unit(u + 2)
                 i, on = divmod(u - 7, 1)
@@ -390,5 +430,4 @@ def tile_biboattention_pa_t_kernel(
                     build_tables(*later[i])
             finish(u)
             if u == 0:
-                build_tables(0, UNIT, GROUP)
                 quantise_unit(2)

@@ -88,7 +88,6 @@ def tile_biboattention_pa_t_kernel(
         operands = {}
         raws = {}
         sumsqs = {}
-        turneds = {}
         rstds = {}
         products = {}
         results = {}
@@ -143,24 +142,6 @@ def tile_biboattention_pa_t_kernel(
                         op0=ALU.mult,
                         op1=ALU.mult,
                     )
-
-        def turn_angles(chunk):
-            bank = psum_t.tile([P, 2, GROUP, P], BF16, name="bank")
-            for a in range(2):
-                for t in range(GROUP):
-                    nc.tensor.transpose(bank[:, a, t], angles[chunk][:, a, t], ident_bf16[:])
-            turneds[chunk] = angle_pool.tile([P, 2, GROUP, P], BF16, name="turned")
-            nc.scalar.copy(out=turneds[chunk][:], in_=bank[:])
-
-        def build_table(chunk, t):
-            if chunk not in tables:
-                tables[chunk] = table_pool.tile([P, GROUP, NORMS, 2, HD], F32, name="table")
-            bank = psum_t.tile([P, 2, NORMS, HD], F32, name="bank")
-            for a in range(2):
-                nc.tensor.matmul(
-                    out=bank[:, a], lhsT=turneds[chunk][:, a, t], rhs=weighted[:, a], start=True, stop=True
-                )
-            nc.scalar.copy(out=tables[chunk][:, t], in_=bank[:].rearrange("p a n d -> p n a d"))
 
         def load_rows(u, parts=1):
             n = u // UNITS_PER_GROUP
@@ -327,18 +308,6 @@ def tile_biboattention_pa_t_kernel(
         )
         w_minus = const.tile([P, NORMS, HALF], BF16)
         nc.vector.tensor_scalar_mul(out=w_minus[:], in0=w_rows[:, :, HALF:HD], scalar1=-1.0)
-        weighted = const.tile([P, 2, NORMS, HD], BF16)
-        for out, w, there in (
-            (weighted[:, 0], w_rows[:], 0),
-            (weighted[:, 1, :, 0:HALF], w_rows[:, :, 0:HALF], HALF),
-            (weighted[:, 1, :, HALF:HD], w_minus[:], 0),
-        ):
-            nc.gpsimd.tensor_tensor(
-                out=out,
-                in0=w,
-                in1=ident_bf16[:, there : there + w.shape[2]].unsqueeze(1).to_broadcast([P, NORMS, w.shape[2]]),
-                op=ALU.mult,
-            )
         wq_grouped = const.tile([P, PASSES * Q_HEADS * HD * 4], BF16, align_bytes=64)
         wk_grouped = const.tile([P, PASSES * HD * 4], BF16, align_bytes=64)
         wq_words = wq_grouped[:].bitcast(F32).rearrange("p (g n u) -> p g n u", g=PASSES, u=2)
@@ -399,13 +368,8 @@ def tile_biboattention_pa_t_kernel(
         for u in range(2, 1 + PROJECT_LAG):
             front(u, [nc.scalar.copy, nc.scalar.copy])
         later = [
-            (chunk, t, t + 1, parts) for chunk in [2] for t in range(GROUP) for parts in ((0,), (1, 2))
+            (chunk, t, t + 1, parts) for chunk in range(G_CHUNK + 1, CHUNKS) for t in range(GROUP) for parts in ((0,), (1, 2))
         ]
-        jobs = {}
-        for i, chunk in enumerate([3]):
-            jobs[8 + i * 2 * (GROUP + 1)] = (turn_angles, (chunk,))
-            for t in range(GROUP):
-                jobs[8 + (i * (GROUP + 1) + t + 1) * 2] = (build_table, (chunk, t))
         for u in range(UNITS):
             ahead = u + 1 + PROJECT_LAG
             if ahead < UNITS:
@@ -420,9 +384,6 @@ def tile_biboattention_pa_t_kernel(
             if u + 1 < UNITS:
                 square_unit(u + 1)
                 norm_unit(u + 1)
-            if u in jobs:
-                job, args = jobs[u]
-                job(*args)
             if u + 2 < UNITS and u > 0:
                 quantise_unit(u + 2)
                 i, on = divmod(u - 7, 1)

import math
from contextlib import ExitStack

import concourse.mybir as mybir
from concourse.masks import make_identity

F32 = mybir.dt.float32
BF16 = mybir.dt.bfloat16
U32 = mybir.dt.uint32
U8 = mybir.dt.uint8
FP8X4 = mybir.dt.float8_e4m3fn_x4
ALU = mybir.AluOpType
ACT = mybir.ActivationFunctionType

P = 128
BATCH = 4
SEQ = 2048
HIDDEN = 1024
Q_HEADS = 2
HEADS = 3
HD = 128
HALF = HD // 2
EPS = 1e-6

K_PASS = 4 * P
PASSES = HIDDEN // K_PASS
WORDS = HIDDEN // 2
BLOCKS = WORDS // P
SLICES = SEQ // P
GROUP = 4
UNIT = 2
CHUNKS = SLICES // GROUP
GROUPS = CHUNKS * BATCH
UNITS_PER_GROUP = GROUP // UNIT
UNITS_PER_CHUNK = BATCH * UNITS_PER_GROUP
UNITS = GROUPS * UNITS_PER_GROUP
LOAD_AHEAD = 10
G_CHUNK = 1
PROJECT_LAG = 2
NORMS = 2

FLOPS = 2 * BATCH * SEQ * HIDDEN * HEADS * HD


def transpose_rows(nc, psum_t, ident, words):
    bank = psum_t.tile([P, WORDS], F32, name="bank")
    for j in range(BLOCKS):
        g, u = divmod(j, 2)
        nc.tensor.transpose(
            bank[:, j * P : (j + 1) * P], words[:, 2 * g * P + u : 2 * (g + 1) * P : 2], ident[:]
        )
    return bank


def copy_grouped(copy, bank, grouped_words):
    copy(
        out=grouped_words,
        in_=bank[:].rearrange("p (g u r) -> p g r u", g=PASSES, u=2),
    )


def tile_biboattention_pa_t_kernel(
    tc, hidden_states, cos, sin, wq, wk, q_norm_w, k_norm_w, ssmax_scale, out_0, out_1
):
    nc = tc.nc
    with ExitStack() as ctx:
        const = ctx.enter_context(tc.tile_pool(name="const", bufs=1))
        x_pool = ctx.enter_context(tc.tile_pool(name="x", bufs=LOAD_AHEAD + 1))
        angle_pool = ctx.enter_context(tc.tile_pool(name="angle", bufs=CHUNKS))
        table_pool = ctx.enter_context(tc.tile_pool(name="table", bufs=CHUNKS))
        mx_pool = ctx.enter_context(tc.tile_pool(name="mx", bufs=4))
        stat_pool = ctx.enter_context(tc.tile_pool(name="stat", bufs=4))
        prod_pool = ctx.enter_context(tc.tile_pool(name="prod", bufs=4))
        out_pool = ctx.enter_context(tc.tile_pool(name="out", bufs=3))
        psum_t = ctx.enter_context(tc.psum_pool(name="psum_t", bufs=3))
        psum_o = ctx.enter_context(tc.psum_pool(name="psum_o", bufs=4))
        psum_w = ctx.enter_context(tc.psum_pool(name="psum_w", bufs=1))
        ctx.enter_context(tc.manual_schedule())

        cos_slices = cos.rearrange("(p t) d -> p t d", t=SLICES)
        sin_slices = sin.rearrange("(p t) d -> p t d", t=SLICES)

        angles = {}
        tables = {}
        x_words = {}
        banks = {}
        groupeds = {}
        operands = {}
        raws = {}
        sumsqs = {}
        rstds = {}
        products = {}
        results = {}

        def group_slices(n):
            chunk = n // BATCH
            return slice(chunk * GROUP, (chunk + 1) * GROUP)

        def load_angles(chunk):
            angle = angle_pool.tile([P, 2, GROUP, HD], BF16)
            nc.sync.dma_start(out=angle[:, 0], in_=cos_slices[:, group_slices(chunk * BATCH), :])
            nc.sync.dma_start(out=angle[:, 1], in_=sin_slices[:, group_slices(chunk * BATCH), :])
            angles[chunk] = angle

        def table_part(chunk, part, t0, t1):
            if chunk not in tables:
                tables[chunk] = table_pool.tile([P, GROUP, NORMS, 2, HD], F32, name="table")
            table, angle = tables[chunk], angles[chunk]
            if part == 0:
                return table[:, t0:t1, :, 0], angle[:, 0, t0:t1]
            here = slice((part - 1) * HALF, part * HALF)
            there = slice((2 - part) * HALF, (3 - part) * HALF)
            return table[:, t0:t1, :, 1, here], angle[:, 1, t0:t1, there]

        def table_product(engine, out, w, angle):
            shape = [P, out.shape[1], NORMS, out.shape[3]]
            engine.tensor_tensor(
                out=out,
                in0=w.unsqueeze(1).to_broadcast(shape),
                in1=angle.unsqueeze(2).to_broadcast(shape),
                op=ALU.mult,
            )

        def build_tables_gpsimd(chunk, v):
            for part, w in enumerate((w_rows[:], w_rows[:, :, 0:HALF], w_minus[:])):
                out, angle = table_part(chunk, part, v * UNIT, (v + 1) * UNIT)
                table_product(nc.gpsimd, out, w, angle)

        def build_tables(chunk, t0, t1, parts=(0, 1, 2)):
            for part in parts:
                if part < 2:
                    out, angle = table_part(chunk, part, t0, t1)
                    table_product(nc.vector, out, w_psum if part == 0 else w_psum[:, :, 0:HALF], angle)
                    continue
                for t in range(t0, t1):
                    out, angle = table_part(chunk, part, t, t + 1)
                    nc.vector.scalar_tensor_tensor(
                        out=out[:, 0],
                        in0=w_psum[:, :, HALF:HD],
                        scalar=-1.0,
                        in1=angle.to_broadcast([P, NORMS, HALF]),
                        op0=ALU.mult,
                        op1=ALU.mult,
                    )

        def load_rows(u, parts=1):
            n = u // UNITS_PER_GROUP
            first = (n // BATCH) * GROUP + (u % UNITS_PER_GROUP) * UNIT
            x_rows = x_pool.tile([P, UNIT * HIDDEN], BF16)
            views = (
                x_rows[:].rearrange("p (t k) -> p t k", t=UNIT),
                hidden_states[n % BATCH].rearrange("(p t) k -> p t k", t=SLICES)[:, first : first + UNIT, :],
            )
            step = UNIT // parts
            for t in range(0, UNIT, step):
                nc.sync.dma_start(out=views[0][:, t : t + step], in_=views[1][:, t : t + step])
            x_words[u] = x_rows[:].bitcast(F32)

        def transpose_slice(u, s):
            if s == 0:
                banks[u] = []
            banks[u].append(transpose_rows(nc, psum_t, ident, x_words[u][:, s * WORDS : (s + 1) * WORDS]))

        def transpose_unit(u):
            for s in range(UNIT):
                transpose_slice(u, s)

        def copy_slice(u, s, copy):
            if s == 0:
                groupeds[u] = mx_pool.tile([P, UNIT * HIDDEN], BF16, align_bytes=64, name="grouped")
            grouped_words = groupeds[u][:].bitcast(F32).rearrange(
                "p (s g r u) -> p s g r u", s=UNIT, g=PASSES, u=2
            )
            copy_grouped(copy, banks[u][s], grouped_words[:, s])

        def quantise_unit(u):
            codes = mx_pool.tile([P, UNIT * PASSES * P], U32, align_bytes=64)
            scales = mx_pool.tile([P, UNIT * PASSES * P], U8, align_bytes=64)
            nc.vector.quantize_mx(out=codes[:].bitcast(FP8X4), scales=scales[:], in_=groupeds[u][:])
            operands[u] = (codes, scales)

        def project_unit(u):
            codes, scales = operands[u]
            raws[u] = []
            for s in range(UNIT):
                raw = psum_o.tile([P, HEADS * HD], F32)
                for cols, w_codes, w_scales, width in projections:
                    for g in range(PASSES):
                        tokens = slice((s * PASSES + g) * P, (s * PASSES + g + 1) * P)
                        features = slice(g * width, (g + 1) * width)
                        nc.tensor.matmul_mx(
                            out=raw[:, cols],
                            lhsT=codes[:, tokens].bitcast(FP8X4),
                            lhsT_scale=scales[:, tokens],
                            rhs=w_codes[:, features].bitcast(FP8X4),
                            rhs_scale=w_scales[:, features],
                            start=(g == 0),
                            stop=(g == PASSES - 1),
                        )
                raws[u].append(raw)

        def square_unit(u, slices=range(UNIT)):
            if slices[0] == 0:
                sumsqs[u] = stat_pool.tile([P, HEADS, UNIT], F32, name="sumsq")
            sumsq = sumsqs[u]
            for s in slices:
                squares = stat_pool.tile([P, HEADS * HD], BF16)
                for h in range(HEADS):
                    head = slice(h * HD, (h + 1) * HD)
                    nc.scalar.activation(
                        out=squares[:, head],
                        in_=raws[u][s][:, head],
                        func=ACT.Square,
                        accum_out=sumsq[:, h, s : s + 1],
                    )

        def norm_unit(u):
            rstd = stat_pool.tile([P, HEADS, UNIT], F32)
            nc.scalar.activation(
                out=rstd[:], in_=sumsqs[u][:], func=ACT.Abs_reciprocal_sqrt, bias=eps[:], scale=1.0 / HD
            )
            rstds[u] = rstd

        def rotate_unit(u):
            table = tables[u // UNITS_PER_CHUNK]
            first = (u % UNITS_PER_GROUP) * UNIT
            product = prod_pool.tile([P, HEADS, UNIT, 2, HD], F32)
            factor = stat_pool.tile([P, Q_HEADS, UNIT], F32)
            nc.vector.tensor_tensor(out=factor[:], in0=gain_psum, in1=rstds[u][:, 0:Q_HEADS], op=ALU.mult)
            factors = [factor[:, 0], factor[:, 1], rstds[u][:, Q_HEADS]]
            for s in range(UNIT):
                for h in (2, 0, 1):
                    nc.vector.scalar_tensor_tensor(
                        out=product[:, h, s],
                        in0=raws[u][s][:, h * HD : (h + 1) * HD].unsqueeze(1).to_broadcast([P, 2, HD]),
                        scalar=factors[h][:, s : s + 1],
                        in1=table[:, first + s, h // Q_HEADS],
                        op0=ALU.mult,
                        op1=ALU.mult,
                    )
            products[u] = product

        def add_slices(engine, u, s0, s1):
            n = u // UNITS_PER_GROUP
            first = (u % UNITS_PER_GROUP) * UNIT
            if first + s0 == 0:
                results[n] = out_pool.tile([P, HEADS, GROUP, HD], F32, name="result")
            terms = products[u][:, :, s0:s1].rearrange("p h s a (i d) -> p h s a i d", i=2)
            engine.tensor_tensor(
                out=results[n][:, :, first + s0 : first + s1, :].rearrange("p h s (i d) -> p h s i d", i=2),
                in0=terms[:, :, :, 0],
                in1=terms[:, :, :, 1, ::-1],
                op=ALU.add,
            )

        def store(n, t0, t1):
            b = n % BATCH
            first = group_slices(n).start
            nc.sync.dma_start(
                out=out_0[b].rearrange("h (p t) d -> p h t d", t=SLICES)[:, :, first + t0 : first + t1, :],
                in_=results[n][:, 0:Q_HEADS, t0:t1],
            )
            nc.sync.dma_start(
                out=out_1[b, 0].rearrange("(p t) d -> p t d", t=SLICES)[:, first + t0 : first + t1, :],
                in_=results[n][:, Q_HEADS, t0:t1],
            )

        def copy_weight(h, copy):
            bank = transpose_rows(nc, psum_t, ident, w_raw[:, h].bitcast(F32))
            if h < Q_HEADS:
                copy_grouped(copy, bank, wq_words[:, :, h * HD : (h + 1) * HD, :])
            else:
                copy_grouped(copy, bank, wk_words)

        w_raw = const.tile([P, HEADS, HIDDEN], BF16)
        for h in range(Q_HEADS):
            nc.sync.dma_start(out=w_raw[:, h], in_=wq[h * HD : (h + 1) * HD, :])
        nc.sync.dma_start(out=w_raw[:, Q_HEADS], in_=wk)
        w_rows = const.tile([P, NORMS, HD], BF16)
        nc.scalar.dma_start(out=w_rows[:, 0], in_=q_norm_w.partition_broadcast(P))
        nc.scalar.dma_start(out=w_rows[:, 1], in_=k_norm_w.partition_broadcast(P))
        gain_rows = const.tile([P, Q_HEADS], BF16)
        nc.scalar.dma_start(
            out=gain_rows[:], in_=ssmax_scale.rearrange("a h b c -> (a h b c)").partition_broadcast(P)
        )
        load_rows(0, UNIT)
        load_angles(0)
        for u in range(1, 4):
            load_rows(u)
        load_angles(G_CHUNK)
        for u in range(4, LOAD_AHEAD):
            load_rows(u)
        for chunk in range(G_CHUNK + 1, CHUNKS):
            load_angles(chunk)
        ident = const.tile([P, P], F32)
        make_identity(nc, ident[:])
        eps = const.tile([P, 1], F32)
        nc.vector.memset(eps[:], EPS)
        warm = const.tile([P, 1], F32)
        nc.scalar.activation(out=warm[:], in_=eps[:], func=ACT.Abs_reciprocal_sqrt)
        ident_bf16 = const.tile([P, P], BF16)
        nc.vector.tensor_copy(out=ident_bf16[:], in_=ident[:])
        row = const.tile([P, Q_HEADS * UNIT], F32)
        nc.vector.tensor_scalar_mul(
            out=row[:].rearrange("p (h s) -> p h s", h=Q_HEADS),
            in0=gain_rows[:].unsqueeze(2).to_broadcast([P, Q_HEADS, UNIT]),
            scalar1=math.log(SEQ),
        )
        w_minus = const.tile([P, NORMS, HALF], BF16)
        nc.vector.tensor_scalar_mul(out=w_minus[:], in0=w_rows[:, :, HALF:HD], scalar1=-1.0)
        wq_grouped = const.tile([P, PASSES * Q_HEADS * HD * 4], BF16, align_bytes=64)
        wk_grouped = const.tile([P, PASSES * HD * 4], BF16, align_bytes=64)
        wq_words = wq_grouped[:].bitcast(F32).rearrange("p (g n u) -> p g n u", g=PASSES, u=2)
        wk_words = wk_grouped[:].bitcast(F32).rearrange("p (g n u) -> p g n u", g=PASSES, u=2)
        wq_codes = const.tile([P, PASSES * Q_HEADS * HD], U32, align_bytes=64)
        wq_scales = const.tile([P, PASSES * Q_HEADS * HD], U8, align_bytes=64)
        wk_codes = const.tile([P, PASSES * HD], U32, align_bytes=64)
        wk_scales = const.tile([P, PASSES * HD], U8, align_bytes=64)
        projections = (
            (slice(0, Q_HEADS * HD), wq_codes, wq_scales, Q_HEADS * HD),
            (slice(Q_HEADS * HD, HEADS * HD), wk_codes, wk_scales, HD),
        )
        copy_weight(0, nc.scalar.copy)
        copy_weight(1, nc.vector.tensor_copy)
        copy_weight(2, nc.vector.tensor_copy)
        nc.vector.quantize_mx(out=wq_codes[:].bitcast(FP8X4), scales=wq_scales[:], in_=wq_grouped[:])
        nc.vector.quantize_mx(out=wk_codes[:].bitcast(FP8X4), scales=wk_scales[:], in_=wk_grouped[:])

        def front(u, copies):
            if u + LOAD_AHEAD < UNITS:
                load_rows(u + LOAD_AHEAD)
            transpose_unit(u)
            for s in range(UNIT):
                copy_slice(u, s, copies[s])

        def finish(u):
            n, v = divmod(u, UNITS_PER_GROUP)
            rotate_unit(u)
            if u < UNITS - 1:
                add_slices(nc.gpsimd, u, 0, UNIT)
                if n == GROUPS - 1:
                    store(n, v * UNIT, (v + 1) * UNIT)
                elif v == UNITS_PER_GROUP - 1:
                    store(n, 0, GROUP)
            else:
                for s in range(UNIT):
                    add_slices(nc.vector, u, s, s + 1)
                    store(n, v * UNIT + s, v * UNIT + s + 1)

        front(0, [nc.scalar.copy, nc.vector.tensor_copy])
        const_bank = psum_w.tile([P, NORMS * HD + Q_HEADS * UNIT], F32)
        nc.tensor.matmul(
            out=const_bank[:, 0 : NORMS * HD].rearrange("p (n d) -> p n d", n=NORMS), lhsT=ident_bf16[:], rhs=w_rows[:], start=True, stop=True
        )
        nc.tensor.matmul(out=const_bank[:, NORMS * HD :], lhsT=ident[:], rhs=row[:], start=True, stop=True)
        w_psum = const_bank[:, 0 : NORMS * HD].rearrange("p (n d) -> p n d", n=NORMS)
        gain_psum = const_bank[:, NORMS * HD :].rearrange("p (h s) -> p h s", h=Q_HEADS)
        quantise_unit(0)
        build_tables(0, 0, UNIT)
        for v in range(UNITS_PER_GROUP):
            build_tables_gpsimd(G_CHUNK, v)
        front(1, [nc.scalar.copy, nc.scalar.copy])
        project_unit(0)
        square_unit(0)
        norm_unit(0)
        quantise_unit(1)
        build_tables(0, UNIT, GROUP)
        for u in range(2, 1 + PROJECT_LAG):
            front(u, [nc.scalar.copy, nc.scalar.copy])
        later = [
            (chunk, t, t + 1, parts) for chunk in range(G_CHUNK + 1, CHUNKS) for t in range(GROUP) for parts in ((0,), (1, 2))
        ]
        for u in range(UNITS):
            ahead = u + 1 + PROJECT_LAG
            if ahead < UNITS:
                if ahead + LOAD_AHEAD < UNITS:
                    load_rows(ahead + LOAD_AHEAD)
                transpose_unit(ahead)
                copy_slice(ahead, 0, nc.scalar.copy)
            if u + 1 < UNITS:
                project_unit(u + 1)
            if ahead < UNITS:
                copy_slice(ahead, 1, nc.scalar.copy)
            if u + 1 < UNITS:
                square_unit(u + 1)
                norm_unit(u + 1)
            if u + 2 < UNITS and u > 0:
                quantise_unit(u + 2)
                i, on = divmod(u - 7, 1)
                if on == 0 and 0 <= i < len(later):
                    build_tables(*later[i])
            finish(u)
            if u == 0:
                quantise_unit(2)
